import numpy as np
import ml_dtypes


def mxq(x, axis, fmt="e4m3"):
    dtype, down = {"e4m3": (ml_dtypes.float8_e4m3fn, 7), "e5m2": (ml_dtypes.float8_e5m2, 14)}[fmt]
    v = np.moveaxis(np.asarray(x, np.float32).astype(ml_dtypes.bfloat16).astype(np.float64), axis, -1)
    blocks = v.reshape(v.shape[:-1] + (-1, 32))
    amax = np.abs(blocks).max(-1, keepdims=True)
    byte = np.maximum(np.where(amax > 0, np.frexp(amax)[1] - 1 + 127, 0) - down, 1)
    scale = np.exp2(byte - 127.0)
    codes = (blocks / scale).astype(np.float32).astype(dtype).astype(np.float64)
    return np.moveaxis((codes * scale).reshape(v.shape), -1, axis)


WIDE = False


def mx_kscale(k):
    if not WIDE:
        return np.ones(k)
    levels = np.array([10, -10, 5, -5, 0])
    a = np.random.permutation(np.resize(levels, k // 512 * 4)).reshape(k // 512, 4)
    idx = np.arange(k)
    return np.exp2(a[idx // 512, idx % 128 // 32])


BF16 = ml_dtypes.bfloat16


def bf(x):
    return np.asarray(x, np.float32).astype(BF16)


def f64(x):
    return np.asarray(x).astype(np.float64)


OBS, H1, H2, ACT, B = 64, 20, 512, 128, 2048
G = 4 * H2


def sigmoid(v):
    return 1.0 / (1.0 + np.exp(-v))


def setup_inputs():
    s = mx_kscale(H2)
    return {
        "h_fc2": bf(np.maximum(np.random.standard_normal((B, H2)), 0.0) * s),
        "hx": bf(np.random.standard_normal((B, H2)) * 0.5 * s),
        "cx": bf(np.random.standard_normal((B, H2)) * 0.8),
        "w_ih": bf(np.random.standard_normal((G, H2)) / np.sqrt(H2) / s),
        "w_hh": bf(np.random.standard_normal((G, H2)) / np.sqrt(H2) / s),
        "b_ih": bf(np.random.standard_normal(G) * 0.2),
        "b_hh": bf(np.random.standard_normal(G) * 0.2),
        "fc3_w": bf(np.random.standard_normal((ACT, H2)) * 3.0 / np.sqrt(H2)),
        "fc3_b": bf(np.random.standard_normal(ACT) * 0.3),
    }


def reference(h_fc2, hx, cx, w_ih, w_hh, b_ih, b_hh, fc3_w, fc3_b):
    gates = ((mxq(f64(h_fc2), 1, "e4m3") @ mxq(f64(w_ih), 1, "e4m3").T) + f64(b_ih)
             + (mxq(f64(hx), 1, "e4m3") @ mxq(f64(w_hh), 1, "e4m3").T) + f64(b_hh))
    i, f, g, o = np.split(gates, 4, axis=-1)
    i, f, o = sigmoid(i), sigmoid(f), sigmoid(o)
    g = np.tanh(g)
    cx_new = f * f64(cx) + i * g
    hx_new = o * np.tanh(cx_new)
    act = np.tanh((mxq(hx_new, 1, "e4m3") @ mxq(f64(fc3_w), 1, "e4m3").T) + f64(fc3_b))
    return act, hx_new, cx_new

@@ -1,0 +1,314 @@
+from contextlib import ExitStack
+
+import concourse.mybir as mybir
+from concourse.masks import make_identity
+
+F32 = mybir.dt.float32
+BF16 = mybir.dt.bfloat16
+U32 = mybir.dt.uint32
+U8 = mybir.dt.uint8
+FP8X4 = mybir.dt.float8_e4m3fn_x4
+FUNC = mybir.ActivationFunctionType
+ALU = mybir.AluOpType
+
+P = 128
+PACK = 4
+HID = 512
+BATCH = 2048
+ACTIONS = 128
+CHUNK = 512
+N_CHUNKS = BATCH // CHUNK
+TILES = CHUNK // P
+GATE_I, GATE_F, GATE_G, GATE_O = 0, 1, 2, 3
+
+FLOPS = 2 * BATCH * (4 * HID) * HID * 2 + 2 * BATCH * ACTIONS * HID
+
+
+def tile_actor_pa_kernel(
+    tc, h_fc2, hx, cx, w_ih, w_hh, b_ih, b_hh, fc3_w, fc3_b, out_0, out_1, out_2
+):
+    nc = tc.nc
+    with ExitStack() as stack:
+        const = stack.enter_context(tc.tile_pool(name="const", bufs=1))
+        loaded = stack.enter_context(tc.tile_pool(name="loaded", bufs=1))
+        operands = stack.enter_context(tc.tile_pool(name="operands", bufs=1))
+        stage = stack.enter_context(tc.tile_pool(name="stage", bufs=4))
+        gates_t = stack.enter_context(tc.tile_pool(name="gates_t", bufs=1))
+        results = stack.enter_context(tc.tile_pool(name="results", bufs=2))
+        head = stack.enter_context(tc.tile_pool(name="head", bufs=1))
+        psum_mx = stack.enter_context(tc.psum_pool(name="psum_mx", bufs=3))
+        psum_tr = stack.enter_context(tc.psum_pool(name="psum_tr", bufs=5))
+        stack.enter_context(tc.manual_schedule())
+
+        def load_rows(name, rows, pattern):
+            raw = loaded.tile([P, TILES, HID], BF16, name=name)
+            if pattern == "batch":
+                nc.sync.dma_start(out=raw[:], in_=rows.rearrange("(p t) k -> p t k", t=TILES))
+            else:
+                nc.sync.dma_start(out=raw[:], in_=rows.rearrange("(t p) k -> p t k", p=P))
+            return raw
+
+        def chunk_rows(c):
+            return slice(c * CHUNK, (c + 1) * CHUNK)
+
+        def gate_rows(gate):
+            return slice(gate * HID, (gate + 1) * HID)
+
+        bias_rows = const.tile([P, P], BF16)
+        nc.vector.memset(bias_rows[:], 0.0)
+        nc.scalar.dma_start(out=bias_rows[0:16, :], in_=b_ih.rearrange("(r c) -> r c", c=P))
+        nc.scalar.dma_start(out=bias_rows[16:32, :], in_=b_hh.rearrange("(r c) -> r c", c=P))
+        fc3_raw = const.tile([P, HID], BF16)
+        nc.scalar.dma_start(out=fc3_raw[:], in_=fc3_w)
+        fc3_bias = const.tile([P, ACTIONS], BF16)
+        nc.scalar.dma_start(out=fc3_bias[:], in_=fc3_b.partition_broadcast(P))
+
+        raw_x = {}
+        raw_w = {}
+        raw_cx = {}
+        raw_x[0] = (
+            load_rows("raw_in0", h_fc2[chunk_rows(0), :], "batch"),
+            load_rows("raw_hx0", hx[chunk_rows(0), :], "batch"),
+        )
+        for gate in (GATE_F, GATE_I, GATE_G, GATE_O):
+            raw_w[gate] = (
+                load_rows("raw_wih%d" % gate, w_ih[gate_rows(gate), :], "gate"),
+                load_rows("raw_whh%d" % gate, w_hh[gate_rows(gate), :], "gate"),
+            )
+            if gate == GATE_I:
+                raw_cx[0] = load_rows("raw_cx0", cx[chunk_rows(0), :], "batch")
+        for c in range(1, N_CHUNKS):
+            raw_x[c] = (
+                load_rows("raw_in%d" % c, h_fc2[chunk_rows(c), :], "batch"),
+                load_rows("raw_hx%d" % c, hx[chunk_rows(c), :], "batch"),
+            )
+            raw_cx[c] = load_rows("raw_cx%d" % c, cx[chunk_rows(c), :], "batch")
+
+        ident_f32 = const.tile([P, P], F32)
+        make_identity(nc, ident_f32[:])
+        ident_bf16 = const.tile([P, P], BF16)
+        make_identity(nc, ident_bf16[:])
+
+        warm = const.tile([P, 1], F32)
+        nc.vector.memset(warm[:], 0.0)
+        nc.scalar.activation(out=warm[:], in_=warm[:], func=FUNC.Sigmoid)
+
+        def empty_bank(engine, out, in_):
+            if engine == "scalar":
+                nc.scalar.copy(out=out, in_=in_)
+            else:
+                nc.vector.tensor_copy(out=out, in_=in_)
+
+        def regroup(raw, engines):
+            words = raw[:].rearrange("p t k -> p (t k)").bitcast(F32)
+            words = words.rearrange("p (t w) -> p t w", t=TILES)
+            grouped = stage.tile([P, CHUNK * PACK], BF16, align_bytes=64, tag="grouped", name="grouped")
+            grouped_words = grouped[:].bitcast(F32).rearrange("p (r u) -> p r u", u=2)
+            for half in range(2):
+                bank = psum_tr.tile([P, 2, 2 * P], F32, tag="tr", name="word_bank")
+                for u in range(2):
+                    for j in range(2):
+                        nc.tensor.transpose(
+                            bank[:, u, j * P : (j + 1) * P],
+                            words[:, 2 * half + j, u * P : (u + 1) * P],
+                            ident_f32[:],
+                        )
+                empty_bank(
+                    engines[half],
+                    grouped_words[:, half * 2 * P : (half + 1) * 2 * P, :],
+                    bank[:].rearrange("p u r -> p r u"),
+                )
+            return grouped
+
+        def quantise(grouped, name, columns):
+            codes = operands.tile([P, columns], U32, align_bytes=64, name="codes_" + name)
+            scales = operands.tile([P, columns], U8, align_bytes=64, name="scales_" + name)
+            nc.vector.quantize_mx(out=codes[:].bitcast(FP8X4), scales=scales[:], in_=grouped[:])
+            return codes, scales
+
+        def prepare_pair(raws, name, engines):
+            grouped = [regroup(raw, engines) for raw in raws]
+            return [quantise(g, "%s_%d" % (name, n), CHUNK) for n, g in enumerate(grouped)]
+
+        x_mx = {}
+        w_mx = {}
+
+        gate_t = {}
+        cell = {}
+        hidden = {}
+        hidden_mx = {}
+
+        def gates(c, gate, func):
+            out_t = gates_t.tile([P, TILES, CHUNK], F32, name="gate_t%d" % gate)
+            for ht in range(TILES):
+                cols = slice(ht * P, (ht + 1) * P)
+                bank = psum_mx.tile([P, CHUNK], F32, tag="mx", name="gate_bank")
+                for n in range(2):
+                    nc.tensor.matmul_mx(
+                        out=bank[:],
+                        lhsT=w_mx[gate][n][0][:, cols].bitcast(FP8X4),
+                        lhsT_scale=w_mx[gate][n][1][:, cols],
+                        rhs=x_mx[c][n][0][:].bitcast(FP8X4),
+                        rhs_scale=x_mx[c][n][1][:],
+                        start=(n == 0),
+                        stop=(n == 1),
+                    )
+                k = gate * TILES + ht
+                nc.scalar.activation(
+                    out=out_t[:, ht, :], in_=bank[:], func=func, bias=gate_bias[:, k : k + 1]
+                )
+            gate_t[gate] = out_t
+
+        def turn_back(source_t, t):
+            bank = psum_tr.tile([P, HID], F32, tag="tr", name="turned_bank")
+            for ht in range(TILES):
+                nc.tensor.transpose(
+                    bank[:, ht * P : (ht + 1) * P], source_t[:, ht, t * P : (t + 1) * P], ident_f32[:]
+                )
+            return bank
+
+        def forget_old_cell(c):
+            cell[c] = results.tile([P, TILES, HID], F32, name="cell")
+            for t in range(TILES):
+                bank = turn_back(gate_t[GATE_F], t)
+                nc.vector.tensor_tensor(
+                    out=cell[c][:, t, :], in0=bank[:], in1=raw_cx[c][:, t, :], op=ALU.mult
+                )
+
+        def input_times_candidate():
+            for ht in range(TILES):
+                nc.vector.tensor_tensor(
+                    out=gate_t[GATE_I][:, ht, :],
+                    in0=gate_t[GATE_I][:, ht, :],
+                    in1=gate_t[GATE_G][:, ht, :],
+                    op=ALU.mult,
+                )
+
+        def new_cell(c):
+            for t in range(TILES):
+                bank = turn_back(gate_t[GATE_I], t)
+                nc.vector.tensor_tensor(
+                    out=cell[c][:, t, :], in0=bank[:], in1=cell[c][:, t, :], op=ALU.add
+                )
+            nc.sync.dma_start(
+                out=out_2[chunk_rows(c), :].rearrange("(p t) h -> p t h", t=TILES), in_=cell[c][:]
+            )
+
+        def squash_cell(c):
+            hidden[c] = results.tile([P, TILES, HID], F32, name="hidden")
+            for t in range(TILES):
+                nc.scalar.activation(out=hidden[c][:, t, :], in_=cell[c][:, t, :], func=FUNC.Tanh)
+
+        def new_hidden(c):
+            for t in range(TILES):
+                bank = turn_back(gate_t[GATE_O], t)
+                nc.vector.tensor_tensor(
+                    out=hidden[c][:, t, :], in0=bank[:], in1=hidden[c][:, t, :], op=ALU.mult
+                )
+            nc.sync.dma_start(
+                out=out_1[chunk_rows(c), :].rearrange("(p t) h -> p t h", t=TILES), in_=hidden[c][:]
+            )
+            rounded = head.tile([P, TILES, HID], BF16, name="rounded")
+            nc.vector.tensor_copy(out=rounded[:], in_=hidden[c][:])
+            return rounded
+
+        def regroup_bf16(rows, grouped):
+            bank = psum_tr.tile([P, PACK, P], BF16, tag="tr", name="bf16_bank")
+            for j in range(PACK):
+                nc.tensor.transpose(bank[:, j, :], rows[:, j * P : (j + 1) * P], ident_bf16[:])
+            nc.vector.tensor_copy(out=grouped, in_=bank[:].rearrange("p j r -> p r j"))
+
+        def regroup_hidden(rounded):
+            grouped = head.tile([P, CHUNK * PACK], BF16, align_bytes=64, name="hidden_grouped")
+            view = grouped[:].rearrange("p (r j) -> p r j", j=PACK)
+            for t in range(TILES):
+                regroup_bf16(rounded[:, t, :], view[:, t * P : (t + 1) * P, :])
+            return grouped
+
+        def action_head(c):
+            codes, scales = hidden_mx[c]
+            bank = psum_mx.tile([P, TILES, ACTIONS], F32, tag="mx", name="act_bank")
+            for t in range(TILES):
+                rows = slice(t * P, (t + 1) * P)
+                nc.tensor.matmul_mx(
+                    out=bank[:, t, :],
+                    lhsT=codes[:, rows].bitcast(FP8X4),
+                    lhsT_scale=scales[:, rows],
+                    rhs=fc3_mx[0][:].bitcast(FP8X4),
+                    rhs_scale=fc3_mx[1][:],
+                    start=True,
+                    stop=True,
+                )
+            return bank
+
+        def finish_actions(c, bank):
+            act = results.tile([P, TILES, ACTIONS], F32, name="act")
+            nc.vector.tensor_tensor(
+                out=act[:],
+                in0=bank[:],
+                in1=fc3_bias[:].unsqueeze(1).to_broadcast([P, TILES, ACTIONS]),
+                op=ALU.add,
+            )
+            nc.scalar.activation(out=act[:], in_=act[:], func=FUNC.Tanh)
+            nc.sync.dma_start(
+                out=out_0[chunk_rows(c), :].rearrange("(p t) a -> p t a", t=TILES), in_=act[:]
+            )
+
+        x_mx[0] = prepare_pair(raw_x[0], "x0", ("scalar", "vector"))
+        w_mx[GATE_F] = prepare_pair(raw_w[GATE_F], "w%d" % GATE_F, ("scalar", "vector"))
+
+        bias_bank = psum_tr.tile([P, P], BF16, tag="tr", name="bias_bank")
+        nc.tensor.transpose(bias_bank[:], bias_rows[:], ident_bf16[:])
+        bias_cols = const.tile([P, 32], F32)
+        nc.vector.tensor_copy(out=bias_cols[:], in_=bias_bank[:, 0:32])
+        gate_bias = const.tile([P, 16], F32)
+        nc.vector.tensor_tensor(
+            out=gate_bias[:], in0=bias_cols[:, 0:16], in1=bias_cols[:, 16:32], op=ALU.add
+        )
+
+        fc3_grouped = const.tile([P, ACTIONS * PACK], BF16, align_bytes=64)
+        regroup_bf16(fc3_raw[:], fc3_grouped[:].rearrange("p (r j) -> p r j", j=PACK))
+        fc3_mx = quantise(fc3_grouped, "fc3", ACTIONS)
+
+        for c in range(N_CHUNKS + 1):
+            now = c < N_CHUNKS
+            first = c == 0
+            before = c > 0
+            after = c + 1 < N_CHUNKS
+
+            if now:
+                gates(c, GATE_F, FUNC.Sigmoid)
+            if first:
+                w_mx[GATE_I] = prepare_pair(raw_w[GATE_I], "w%d" % GATE_I, ("scalar", "vector"))
+            if before:
+                rounded = new_hidden(c - 1)
+
+            if now:
+                gates(c, GATE_I, FUNC.Sigmoid)
+            if first:
+                w_mx[GATE_G] = prepare_pair(raw_w[GATE_G], "w%d" % GATE_G, ("scalar", "vector"))
+            if now:
+                forget_old_cell(c)
+            if before:
+                hidden_grouped = regroup_hidden(rounded)
+
+            if now:
+                gates(c, GATE_G, FUNC.Tanh)
+                input_times_candidate()
+            if first:
+                w_mx[GATE_O] = prepare_pair(raw_w[GATE_O], "w%d" % GATE_O, ("scalar", "vector"))
+            if before:
+                hidden_mx[c - 1] = quantise(hidden_grouped, "hidden", CHUNK)
+
+            if now:
+                gates(c, GATE_O, FUNC.Sigmoid)
+            if before:
+                act_bank = action_head(c - 1)
+            if now:
+                new_cell(c)
+            if before:
+                finish_actions(c - 1, act_bank)
+            if after:
+                x_mx[c + 1] = prepare_pair(raw_x[c + 1], "x%d" % (c + 1), ("scalar", "scalar"))
+            if now:
+                squash_cell(c)

@@ -19,7 +19,15 @@ ACTIONS = 128
 CHUNK = 512
 N_CHUNKS = BATCH // CHUNK
 TILES = CHUNK // P
+HALF = TILES // 2
 GATE_I, GATE_F, GATE_G, GATE_O = 0, 1, 2, 3
+GATE_ORDER = (GATE_F, GATE_I, GATE_G, GATE_O)
+GATE_FUNC = {
+    GATE_I: FUNC.Sigmoid,
+    GATE_F: FUNC.Sigmoid,
+    GATE_G: FUNC.Tanh,
+    GATE_O: FUNC.Sigmoid,
+}
 
 FLOPS = 2 * BATCH * (4 * HID) * HID * 2 + 2 * BATCH * ACTIONS * HID
 
@@ -32,27 +40,31 @@ def tile_actor_pa_kernel(
         const = stack.enter_context(tc.tile_pool(name="const", bufs=1))
         loaded = stack.enter_context(tc.tile_pool(name="loaded", bufs=1))
         operands = stack.enter_context(tc.tile_pool(name="operands", bufs=1))
-        stage = stack.enter_context(tc.tile_pool(name="stage", bufs=4))
+        stage = stack.enter_context(tc.tile_pool(name="stage", bufs=6))
         gates_t = stack.enter_context(tc.tile_pool(name="gates_t", bufs=1))
         results = stack.enter_context(tc.tile_pool(name="results", bufs=2))
-        head = stack.enter_context(tc.tile_pool(name="head", bufs=1))
         psum_mx = stack.enter_context(tc.psum_pool(name="psum_mx", bufs=3))
         psum_tr = stack.enter_context(tc.psum_pool(name="psum_tr", bufs=5))
         stack.enter_context(tc.manual_schedule())
-
-        def load_rows(name, rows, pattern):
-            raw = loaded.tile([P, TILES, HID], BF16, name=name)
-            if pattern == "batch":
-                nc.sync.dma_start(out=raw[:], in_=rows.rearrange("(p t) k -> p t k", t=TILES))
-            else:
-                nc.sync.dma_start(out=raw[:], in_=rows.rearrange("(t p) k -> p t k", p=P))
-            return raw
 
         def chunk_rows(c):
             return slice(c * CHUNK, (c + 1) * CHUNK)
 
         def gate_rows(gate):
             return slice(gate * HID, (gate + 1) * HID)
+
+        def tiles_of(half):
+            return range(half * HALF, (half + 1) * HALF)
+
+        def load_batch_rows(name, rows):
+            raw = loaded.tile([P, TILES, HID], BF16, name=name)
+            nc.sync.dma_start(out=raw[:], in_=rows.rearrange("(p t) k -> p t k", t=TILES))
+            return raw
+
+        def load_gate_rows(name, rows):
+            raw = loaded.tile([P, TILES, HID], BF16, name=name)
+            nc.sync.dma_start(out=raw[:], in_=rows.rearrange("(t p) k -> p t k", p=P))
+            return raw
 
         bias_rows = const.tile([P, P], BF16)
         nc.vector.memset(bias_rows[:], 0.0)
@@ -66,23 +78,33 @@ def tile_actor_pa_kernel(
         raw_x = {}
         raw_w = {}
         raw_cx = {}
-        raw_x[0] = (
-            load_rows("raw_in0", h_fc2[chunk_rows(0), :], "batch"),
-            load_rows("raw_hx0", hx[chunk_rows(0), :], "batch"),
-        )
-        for gate in (GATE_F, GATE_I, GATE_G, GATE_O):
-            raw_w[gate] = (
-                load_rows("raw_wih%d" % gate, w_ih[gate_rows(gate), :], "gate"),
-                load_rows("raw_whh%d" % gate, w_hh[gate_rows(gate), :], "gate"),
-            )
-            if gate == GATE_I:
-                raw_cx[0] = load_rows("raw_cx0", cx[chunk_rows(0), :], "batch")
-        for c in range(1, N_CHUNKS):
+
+        def load_chunk(c):
             raw_x[c] = (
-                load_rows("raw_in%d" % c, h_fc2[chunk_rows(c), :], "batch"),
-                load_rows("raw_hx%d" % c, hx[chunk_rows(c), :], "batch"),
+                load_batch_rows("raw_in%d" % c, h_fc2[chunk_rows(c), :]),
+                load_batch_rows("raw_hx%d" % c, hx[chunk_rows(c), :]),
             )
-            raw_cx[c] = load_rows("raw_cx%d" % c, cx[chunk_rows(c), :], "batch")
+
+        def load_old_cell(c):
+            raw_cx[c] = load_batch_rows("raw_cx%d" % c, cx[chunk_rows(c), :])
+
+        def load_gate(gate):
+            raw_w[gate] = (
+                load_gate_rows("raw_wih%d" % gate, w_ih[gate_rows(gate), :]),
+                load_gate_rows("raw_whh%d" % gate, w_hh[gate_rows(gate), :]),
+            )
+
+        load_chunk(0)
+        load_gate(GATE_F)
+        load_gate(GATE_I)
+        load_gate(GATE_G)
+        load_old_cell(0)
+        load_chunk(1)
+        load_gate(GATE_O)
+        for c in range(1, N_CHUNKS):
+            if c + 1 < N_CHUNKS:
+                load_chunk(c + 1)
+            load_old_cell(c)
 
         ident_f32 = const.tile([P, P], F32)
         make_identity(nc, ident_f32[:])
@@ -93,54 +115,61 @@ def tile_actor_pa_kernel(
         nc.vector.memset(warm[:], 0.0)
         nc.scalar.activation(out=warm[:], in_=warm[:], func=FUNC.Sigmoid)
 
-        def empty_bank(engine, out, in_):
-            if engine == "scalar":
-                nc.scalar.copy(out=out, in_=in_)
-            else:
-                nc.vector.tensor_copy(out=out, in_=in_)
-
-        def regroup(raw, engines):
-            words = raw[:].rearrange("p t k -> p (t k)").bitcast(F32)
-            words = words.rearrange("p (t w) -> p t w", t=TILES)
-            grouped = stage.tile([P, CHUNK * PACK], BF16, align_bytes=64, tag="grouped", name="grouped")
-            grouped_words = grouped[:].bitcast(F32).rearrange("p (r u) -> p r u", u=2)
-            for half in range(2):
-                bank = psum_tr.tile([P, 2, 2 * P], F32, tag="tr", name="word_bank")
-                for u in range(2):
-                    for j in range(2):
-                        nc.tensor.transpose(
-                            bank[:, u, j * P : (j + 1) * P],
-                            words[:, 2 * half + j, u * P : (u + 1) * P],
-                            ident_f32[:],
-                        )
-                empty_bank(
-                    engines[half],
-                    grouped_words[:, half * 2 * P : (half + 1) * 2 * P, :],
-                    bank[:].rearrange("p u r -> p r u"),
-                )
-            return grouped
-
-        def quantise(grouped, name, columns):
+        def new_operand(name, columns):
             codes = operands.tile([P, columns], U32, align_bytes=64, name="codes_" + name)
             scales = operands.tile([P, columns], U8, align_bytes=64, name="scales_" + name)
-            nc.vector.quantize_mx(out=codes[:].bitcast(FP8X4), scales=scales[:], in_=grouped[:])
             return codes, scales
 
-        def prepare_pair(raws, name, engines):
-            grouped = [regroup(raw, engines) for raw in raws]
-            return [quantise(g, "%s_%d" % (name, n), CHUNK) for n, g in enumerate(grouped)]
+        def regroup(raw, half, engine):
+            words = raw[:].rearrange("p t k -> p (t k)").bitcast(F32)
+            words = words.rearrange("p (t w) -> p t w", t=TILES)
+            bank = psum_tr.tile([P, 2, HALF * P], F32, tag="tr", name="word_bank")
+            for u in range(2):
+                for j, t in enumerate(tiles_of(half)):
+                    nc.tensor.transpose(
+                        bank[:, u, j * P : (j + 1) * P], words[:, t, u * P : (u + 1) * P], ident_f32[:]
+                    )
+            grouped = stage.tile([P, HALF * P * PACK], BF16, align_bytes=64, name="grouped")
+            grouped_words = grouped[:].bitcast(F32).rearrange("p (r u) -> p r u", u=2)
+            if engine == "scalar":
+                nc.scalar.copy(out=grouped_words, in_=bank[:].rearrange("p u r -> p r u"))
+            else:
+                nc.vector.tensor_copy(out=grouped_words, in_=bank[:].rearrange("p u r -> p r u"))
+            return grouped
+
+        def quantise(grouped, operand, half):
+            codes, scales = operand
+            columns = slice(half * HALF * P, (half + 1) * HALF * P)
+            nc.vector.quantize_mx(
+                out=codes[:, columns].bitcast(FP8X4), scales=scales[:, columns], in_=grouped[:]
+            )
 
         x_mx = {}
         w_mx = {}
 
+        def regroup_weights(gate, half):
+            if half == 0:
+                w_mx[gate] = [new_operand("w%d_%d" % (gate, n), HID) for n in range(2)]
+            return [
+                regroup(raw_w[gate][0], half, "scalar"),
+                regroup(raw_w[gate][1], half, "vector"),
+            ]
+
+        def quantise_weights(grouped, gate, half):
+            for n in range(2):
+                quantise(grouped[n], w_mx[gate][n], half)
+
         gate_t = {}
         cell = {}
         hidden = {}
+        rounded = {}
         hidden_mx = {}
+        actions = {}
 
-        def gates(c, gate, func):
-            out_t = gates_t.tile([P, TILES, CHUNK], F32, name="gate_t%d" % gate)
-            for ht in range(TILES):
+        def gate_passes(c, gate, half):
+            if half == 0:
+                gate_t[gate] = gates_t.tile([P, TILES, CHUNK], F32, name="gate_t%d" % gate)
+            for ht in tiles_of(half):
                 cols = slice(ht * P, (ht + 1) * P)
                 bank = psum_mx.tile([P, CHUNK], F32, tag="mx", name="gate_bank")
                 for n in range(2):
@@ -155,9 +184,11 @@ def tile_actor_pa_kernel(
                     )
                 k = gate * TILES + ht
                 nc.scalar.activation(
-                    out=out_t[:, ht, :], in_=bank[:], func=func, bias=gate_bias[:, k : k + 1]
+                    out=gate_t[gate][:, ht, :],
+                    in_=bank[:],
+                    func=GATE_FUNC[gate],
+                    bias=gate_bias[:, k : k + 1],
                 )
-            gate_t[gate] = out_t
 
         def turn_back(source_t, t):
             bank = psum_tr.tile([P, HID], F32, tag="tr", name="turned_bank")
@@ -167,16 +198,22 @@ def tile_actor_pa_kernel(
                 )
             return bank
 
-        def forget_old_cell(c):
-            cell[c] = results.tile([P, TILES, HID], F32, name="cell")
-            for t in range(TILES):
+        def store_half(out, c, half, tile):
+            view = out[chunk_rows(c), :].rearrange("(p t) h -> p t h", t=TILES)
+            part = slice(half * HALF, (half + 1) * HALF)
+            nc.sync.dma_start(out=view[:, part, :], in_=tile[:, part, :])
+
+        def forget_old_cell(c, half):
+            if half == 0:
+                cell[c] = results.tile([P, TILES, HID], F32, name="cell")
+            for t in tiles_of(half):
                 bank = turn_back(gate_t[GATE_F], t)
                 nc.vector.tensor_tensor(
                     out=cell[c][:, t, :], in0=bank[:], in1=raw_cx[c][:, t, :], op=ALU.mult
                 )
 
-        def input_times_candidate():
-            for ht in range(TILES):
+        def input_times_candidate(half):
+            for ht in tiles_of(half):
                 nc.vector.tensor_tensor(
                     out=gate_t[GATE_I][:, ht, :],
                     in0=gate_t[GATE_I][:, ht, :],
@@ -184,54 +221,59 @@ def tile_actor_pa_kernel(
                     op=ALU.mult,
                 )
 
-        def new_cell(c):
-            for t in range(TILES):
+        def new_cell(c, half):
+            for t in tiles_of(half):
                 bank = turn_back(gate_t[GATE_I], t)
                 nc.vector.tensor_tensor(
                     out=cell[c][:, t, :], in0=bank[:], in1=cell[c][:, t, :], op=ALU.add
                 )
-            nc.sync.dma_start(
-                out=out_2[chunk_rows(c), :].rearrange("(p t) h -> p t h", t=TILES), in_=cell[c][:]
-            )
+            store_half(out_2, c, half, cell[c])
 
-        def squash_cell(c):
-            hidden[c] = results.tile([P, TILES, HID], F32, name="hidden")
-            for t in range(TILES):
+        def squash_cell(c, half):
+            if half == 0:
+                hidden[c] = results.tile([P, TILES, HID], F32, name="hidden")
+            for t in tiles_of(half):
                 nc.scalar.activation(out=hidden[c][:, t, :], in_=cell[c][:, t, :], func=FUNC.Tanh)
 
-        def new_hidden(c):
-            for t in range(TILES):
+        def new_hidden(c, half):
+            if half == 0:
+                rounded[c] = results.tile([P, TILES, HID], BF16, name="rounded")
+            for t in tiles_of(half):
                 bank = turn_back(gate_t[GATE_O], t)
                 nc.vector.tensor_tensor(
                     out=hidden[c][:, t, :], in0=bank[:], in1=hidden[c][:, t, :], op=ALU.mult
                 )
-            nc.sync.dma_start(
-                out=out_1[chunk_rows(c), :].rearrange("(p t) h -> p t h", t=TILES), in_=hidden[c][:]
-            )
-            rounded = head.tile([P, TILES, HID], BF16, name="rounded")
-            nc.vector.tensor_copy(out=rounded[:], in_=hidden[c][:])
-            return rounded
+            store_half(out_1, c, half, hidden[c])
+            for t in tiles_of(half):
+                nc.vector.tensor_copy(out=rounded[c][:, t, :], in_=hidden[c][:, t, :])
 
-        def regroup_bf16(rows, grouped):
+        def regroup_bf16(rows, grouped, engine):
             bank = psum_tr.tile([P, PACK, P], BF16, tag="tr", name="bf16_bank")
             for j in range(PACK):
                 nc.tensor.transpose(bank[:, j, :], rows[:, j * P : (j + 1) * P], ident_bf16[:])
-            nc.vector.tensor_copy(out=grouped, in_=bank[:].rearrange("p j r -> p r j"))
+            if engine == "scalar":
+                nc.scalar.copy(out=grouped, in_=bank[:].rearrange("p j r -> p r j"))
+            else:
+                nc.vector.tensor_copy(out=grouped, in_=bank[:].rearrange("p j r -> p r j"))
 
-        def regroup_hidden(rounded):
-            grouped = head.tile([P, CHUNK * PACK], BF16, align_bytes=64, name="hidden_grouped")
+        def regroup_hidden(c, half):
+            grouped = stage.tile([P, HALF * P * PACK], BF16, align_bytes=64, name="grouped")
             view = grouped[:].rearrange("p (r j) -> p r j", j=PACK)
-            for t in range(TILES):
-                regroup_bf16(rounded[:, t, :], view[:, t * P : (t + 1) * P, :])
+            for j, t in enumerate(tiles_of(half)):
+                regroup_bf16(
+                    rounded[c][:, t, :], view[:, j * P : (j + 1) * P, :], ("scalar", "vector")[j]
+                )
             return grouped
 
-        def action_head(c):
+        def action_head(c, half):
+            if half == 0:
+                actions[c] = results.tile([P, TILES, ACTIONS], F32, name="actions")
             codes, scales = hidden_mx[c]
-            bank = psum_mx.tile([P, TILES, ACTIONS], F32, tag="mx", name="act_bank")
-            for t in range(TILES):
+            bank = psum_mx.tile([P, HALF, ACTIONS], F32, tag="mx", name="act_bank")
+            for j, t in enumerate(tiles_of(half)):
                 rows = slice(t * P, (t + 1) * P)
                 nc.tensor.matmul_mx(
-                    out=bank[:, t, :],
+                    out=bank[:, j, :],
                     lhsT=codes[:, rows].bitcast(FP8X4),
                     lhsT_scale=scales[:, rows],
                     rhs=fc3_mx[0][:].bitcast(FP8X4),
@@ -239,23 +281,24 @@ def tile_actor_pa_kernel(
                     start=True,
                     stop=True,
                 )
-            return bank
-
-        def finish_actions(c, bank):
-            act = results.tile([P, TILES, ACTIONS], F32, name="act")
+            part = actions[c][:, half * HALF : (half + 1) * HALF, :]
             nc.vector.tensor_tensor(
-                out=act[:],
+                out=part,
                 in0=bank[:],
-                in1=fc3_bias[:].unsqueeze(1).to_broadcast([P, TILES, ACTIONS]),
+                in1=fc3_bias[:].unsqueeze(1).to_broadcast([P, HALF, ACTIONS]),
                 op=ALU.add,
             )
-            nc.scalar.activation(out=act[:], in_=act[:], func=FUNC.Tanh)
-            nc.sync.dma_start(
-                out=out_0[chunk_rows(c), :].rearrange("(p t) a -> p t a", t=TILES), in_=act[:]
-            )
+            nc.scalar.activation(out=part, in_=part, func=FUNC.Tanh)
+            store_half(out_0, c, half, actions[c])
 
-        x_mx[0] = prepare_pair(raw_x[0], "x0", ("scalar", "vector"))
-        w_mx[GATE_F] = prepare_pair(raw_w[GATE_F], "w%d" % GATE_F, ("scalar", "vector"))
+        x_mx[0] = [new_operand("x0_%d" % n, CHUNK) for n in range(2)]
+        for half in range(2):
+            first_x = [
+                regroup(raw_x[0][0], half, "scalar"),
+                regroup(raw_x[0][1], half, "vector"),
+            ]
+            for n in range(2):
+                quantise(first_x[n], x_mx[0][n], half)
 
         bias_bank = psum_tr.tile([P, P], BF16, tag="tr", name="bias_bank")
         nc.tensor.transpose(bias_bank[:], bias_rows[:], ident_bf16[:])
@@ -266,49 +309,77 @@ def tile_actor_pa_kernel(
             out=gate_bias[:], in0=bias_cols[:, 0:16], in1=bias_cols[:, 16:32], op=ALU.add
         )
 
+        for half in range(2):
+            quantise_weights(regroup_weights(GATE_F, half), GATE_F, half)
+
         fc3_grouped = const.tile([P, ACTIONS * PACK], BF16, align_bytes=64)
-        regroup_bf16(fc3_raw[:], fc3_grouped[:].rearrange("p (r j) -> p r j", j=PACK))
-        fc3_mx = quantise(fc3_grouped, "fc3", ACTIONS)
+        fc3_mx = new_operand("fc3", ACTIONS)
 
         for c in range(N_CHUNKS + 1):
             now = c < N_CHUNKS
             first = c == 0
             before = c > 0
             after = c + 1 < N_CHUNKS
-
-            if now:
-                gates(c, GATE_F, FUNC.Sigmoid)
-            if first:
-                w_mx[GATE_I] = prepare_pair(raw_w[GATE_I], "w%d" % GATE_I, ("scalar", "vector"))
-            if before:
-                rounded = new_hidden(c - 1)
-
-            if now:
-                gates(c, GATE_I, FUNC.Sigmoid)
-            if first:
-                w_mx[GATE_G] = prepare_pair(raw_w[GATE_G], "w%d" % GATE_G, ("scalar", "vector"))
-            if now:
-                forget_old_cell(c)
-            if before:
-                hidden_grouped = regroup_hidden(rounded)
-
-            if now:
-                gates(c, GATE_G, FUNC.Tanh)
-                input_times_candidate()
-            if first:
-                w_mx[GATE_O] = prepare_pair(raw_w[GATE_O], "w%d" % GATE_O, ("scalar", "vector"))
-            if before:
-                hidden_mx[c - 1] = quantise(hidden_grouped, "hidden", CHUNK)
-
-            if now:
-                gates(c, GATE_O, FUNC.Sigmoid)
-            if before:
-                act_bank = action_head(c - 1)
-            if now:
-                new_cell(c)
-            if before:
-                finish_actions(c - 1, act_bank)
             if after:
-                x_mx[c + 1] = prepare_pair(raw_x[c + 1], "x%d" % (c + 1), ("scalar", "scalar"))
-            if now:
-                squash_cell(c)
+                x_mx[c + 1] = [new_operand("x%d_%d" % (c + 1, n), CHUNK) for n in range(2)]
+            if before:
+                hidden_mx[c - 1] = new_operand("hidden", CHUNK)
+
+            for half in range(2):
+                if now:
+                    gate_passes(c, GATE_F, half)
+                if first:
+                    quantise_weights(regroup_weights(GATE_I, half), GATE_I, half)
+                if before and half == 0:
+                    squash_cell(c - 1, 1)
+                if before:
+                    new_hidden(c - 1, half)
+
+            for half in range(2):
+                if now:
+                    gate_passes(c, GATE_I, half)
+                if first:
+                    grouped_w = regroup_weights(GATE_G, half)
+                if now:
+                    forget_old_cell(c, half)
+                if after:
+                    grouped_x = regroup(raw_x[c + 1][0], half, "scalar")
+                if first:
+                    quantise_weights(grouped_w, GATE_G, half)
+                if after:
+                    quantise(grouped_x, x_mx[c + 1][0], half)
+
+            for half in range(2):
+                if now:
+                    gate_passes(c, GATE_G, half)
+                    input_times_candidate(half)
+                if first:
+                    grouped_w = regroup_weights(GATE_O, half)
+                if before:
+                    grouped_h = regroup_hidden(c - 1, half)
+                if after:
+                    grouped_x = regroup(raw_x[c + 1][1], half, "scalar")
+                if first:
+                    quantise_weights(grouped_w, GATE_O, half)
+                if before:
+                    quantise(grouped_h, hidden_mx[c - 1], half)
+                if after:
+                    quantise(grouped_x, x_mx[c + 1][1], half)
+
+            for half in range(2):
+                if now:
+                    gate_passes(c, GATE_O, half)
+                if before:
+                    action_head(c - 1, half)
+                if now and half == 1:
+                    squash_cell(c, 0)
+                if now:
+                    new_cell(c, half)
+
+            if first:
+                regroup_bf16(
+                    fc3_raw[:], fc3_grouped[:].rearrange("p (r j) -> p r j", j=PACK), "vector"
+                )
+                nc.vector.quantize_mx(
+                    out=fc3_mx[0][:].bitcast(FP8X4), scales=fc3_mx[1][:], in_=fc3_grouped[:]
+                )

@@ -247,24 +247,6 @@ def tile_actor_pa_kernel(
             for t in tiles_of(half):
                 nc.vector.tensor_copy(out=rounded[c][:, t, :], in_=hidden[c][:, t, :])
 
-        def regroup_bf16(rows, grouped, engine):
-            bank = psum_tr.tile([P, PACK, P], BF16, tag="tr", name="bf16_bank")
-            for j in range(PACK):
-                nc.tensor.transpose(bank[:, j, :], rows[:, j * P : (j + 1) * P], ident_bf16[:])
-            if engine == "scalar":
-                nc.scalar.copy(out=grouped, in_=bank[:].rearrange("p j r -> p r j"))
-            else:
-                nc.vector.tensor_copy(out=grouped, in_=bank[:].rearrange("p j r -> p r j"))
-
-        def regroup_hidden(c, half):
-            grouped = stage.tile([P, HALF * P * PACK], BF16, align_bytes=64, name="grouped")
-            view = grouped[:].rearrange("p (r j) -> p r j", j=PACK)
-            for j, t in enumerate(tiles_of(half)):
-                regroup_bf16(
-                    rounded[c][:, t, :], view[:, j * P : (j + 1) * P, :], ("scalar", "vector")[j]
-                )
-            return grouped
-
         def action_head(c, half):
             if half == 0:
                 actions[c] = results.tile([P, TILES, ACTIONS], F32, name="actions")
@@ -356,7 +338,7 @@ def tile_actor_pa_kernel(
                 if first:
                     grouped_w = regroup_weights(GATE_O, half)
                 if before:
-                    grouped_h = regroup_hidden(c - 1, half)
+                    grouped_h = regroup(rounded[c - 1], half, "scalar")
                 if after:
                     grouped_x = regroup(raw_x[c + 1][1], half, "scalar")
                 if first:
@@ -377,8 +359,15 @@ def tile_actor_pa_kernel(
                     new_cell(c, half)
 
             if first:
-                regroup_bf16(
-                    fc3_raw[:], fc3_grouped[:].rearrange("p (r j) -> p r j", j=PACK), "vector"
+                fc3_words = fc3_raw[:].bitcast(F32)
+                fc3_bank = psum_tr.tile([P, 2, ACTIONS], F32, tag="tr", name="fc3_bank")
+                for u in range(2):
+                    nc.tensor.transpose(
+                        fc3_bank[:, u, :], fc3_words[:, u * P : (u + 1) * P], ident_f32[:]
+                    )
+                nc.vector.tensor_copy(
+                    out=fc3_grouped[:].bitcast(F32).rearrange("p (r u) -> p r u", u=2),
+                    in_=fc3_bank[:].rearrange("p u r -> p r u"),
                 )
                 nc.vector.quantize_mx(
                     out=fc3_mx[0][:].bitcast(FP8X4), scales=fc3_mx[1][:], in_=fc3_grouped[:]

@@ -70,10 +70,6 @@ def tile_actor_pa_kernel(
         nc.vector.memset(bias_rows[:], 0.0)
         nc.scalar.dma_start(out=bias_rows[0:16, :], in_=b_ih.rearrange("(r c) -> r c", c=P))
         nc.scalar.dma_start(out=bias_rows[16:32, :], in_=b_hh.rearrange("(r c) -> r c", c=P))
-        fc3_raw = const.tile([P, HID], BF16)
-        nc.scalar.dma_start(out=fc3_raw[:], in_=fc3_w)
-        fc3_bias = const.tile([P, ACTIONS], BF16)
-        nc.scalar.dma_start(out=fc3_bias[:], in_=fc3_b.partition_broadcast(P))
 
         raw_x = {}
         raw_w = {}
@@ -105,6 +101,10 @@ def tile_actor_pa_kernel(
             if c + 1 < N_CHUNKS:
                 load_chunk(c + 1)
             load_old_cell(c)
+        fc3_raw = const.tile([P, HID], BF16)
+        nc.sync.dma_start(out=fc3_raw[:], in_=fc3_w)
+        fc3_bias = const.tile([P, ACTIONS], BF16)
+        nc.sync.dma_start(out=fc3_bias[:], in_=fc3_b.partition_broadcast(P))
 
         ident_f32 = const.tile([P, P], F32)
         make_identity(nc, ident_f32[:])
@@ -331,6 +331,21 @@ def tile_actor_pa_kernel(
                 if after:
                     quantise(grouped_x, x_mx[c + 1][0], half)
 
+            if c == 1:
+                fc3_words = fc3_raw[:].bitcast(F32)
+                fc3_bank = psum_tr.tile([P, 2, ACTIONS], F32, tag="tr", name="fc3_bank")
+                for u in range(2):
+                    nc.tensor.transpose(
+                        fc3_bank[:, u, :], fc3_words[:, u * P : (u + 1) * P], ident_f32[:]
+                    )
+                nc.vector.tensor_copy(
+                    out=fc3_grouped[:].bitcast(F32).rearrange("p (r u) -> p r u", u=2),
+                    in_=fc3_bank[:].rearrange("p u r -> p r u"),
+                )
+                nc.vector.quantize_mx(
+                    out=fc3_mx[0][:].bitcast(FP8X4), scales=fc3_mx[1][:], in_=fc3_grouped[:]
+                )
+
             for half in range(2):
                 if now:
                     gate_passes(c, GATE_G, half)
@@ -357,18 +372,3 @@ def tile_actor_pa_kernel(
                     squash_cell(c, 0)
                 if now:
                     new_cell(c, half)
-
-            if first:
-                fc3_words = fc3_raw[:].bitcast(F32)
-                fc3_bank = psum_tr.tile([P, 2, ACTIONS], F32, tag="tr", name="fc3_bank")
-                for u in range(2):
-                    nc.tensor.transpose(
-                        fc3_bank[:, u, :], fc3_words[:, u * P : (u + 1) * P], ident_f32[:]
-                    )
-                nc.vector.tensor_copy(
-                    out=fc3_grouped[:].bitcast(F32).rearrange("p (r u) -> p r u", u=2),
-                    in_=fc3_bank[:].rearrange("p u r -> p r u"),
-                )
-                nc.vector.quantize_mx(
-                    out=fc3_mx[0][:].bitcast(FP8X4), scales=fc3_mx[1][:], in_=fc3_grouped[:]
-                )

@@ -61,15 +61,12 @@ def tile_actor_pa_kernel(
             nc.sync.dma_start(out=raw[:], in_=rows.rearrange("(p t) k -> p t k", t=TILES))
             return raw
 
-        def load_gate_rows(name, rows):
-            raw = loaded.tile([P, TILES, HID], BF16, name=name)
-            nc.sync.dma_start(out=raw[:], in_=rows.rearrange("(t p) k -> p t k", p=P))
-            return raw
-
-        bias_rows = const.tile([P, P], BF16)
+        bias_rows = const.tile([P, HID], BF16)
         nc.vector.memset(bias_rows[:], 0.0)
-        nc.scalar.dma_start(out=bias_rows[0:16, :], in_=b_ih.rearrange("(r c) -> r c", c=P))
-        nc.scalar.dma_start(out=bias_rows[16:32, :], in_=b_hh.rearrange("(r c) -> r c", c=P))
+        nc.scalar.dma_start(out=bias_rows[0:4, :], in_=b_ih.rearrange("(g c) -> g c", c=HID))
+        nc.scalar.dma_start(out=bias_rows[4:8, :], in_=b_hh.rearrange("(g c) -> g c", c=HID))
+        nc.scalar.dma_start(out=bias_rows[8:9, 0:ACTIONS], in_=fc3_b.unsqueeze(0))
+        fc3_raw = const.tile([P, HID], BF16)
 
         raw_x = {}
         raw_w = {}
@@ -84,27 +81,33 @@ def tile_actor_pa_kernel(
         def load_old_cell(c):
             raw_cx[c] = load_batch_rows("raw_cx%d" % c, cx[chunk_rows(c), :])
 
+        def load_in_halves(name, pair, rows):
+            raw = [loaded.tile([P, TILES, HID], BF16, name="%s_%d" % (name, n)) for n in range(2)]
+            for half in range(2):
+                part = slice(half * HALF, (half + 1) * HALF)
+                for n in range(2):
+                    view = pair[n][rows, :].rearrange("(p t) k -> p t k", t=TILES)
+                    nc.sync.dma_start(out=raw[n][:, part, :], in_=view[:, part, :])
+            return raw
+
         def load_gate(gate):
             raw_w[gate] = (
-                load_gate_rows("raw_wih%d" % gate, w_ih[gate_rows(gate), :]),
-                load_gate_rows("raw_whh%d" % gate, w_hh[gate_rows(gate), :]),
+                load_batch_rows("raw_wih%d" % gate, w_ih[gate_rows(gate), :]),
+                load_batch_rows("raw_whh%d" % gate, w_hh[gate_rows(gate), :]),
             )
 
-        load_chunk(0)
-        load_gate(GATE_F)
+        raw_x[0] = load_in_halves("raw_x0", (h_fc2, hx), chunk_rows(0))
+        raw_w[GATE_F] = load_in_halves("raw_wf", (w_ih, w_hh), gate_rows(GATE_F))
         load_gate(GATE_I)
         load_gate(GATE_G)
         load_old_cell(0)
         load_chunk(1)
         load_gate(GATE_O)
+        nc.sync.dma_start(out=fc3_raw[:], in_=fc3_w)
         for c in range(1, N_CHUNKS):
             if c + 1 < N_CHUNKS:
                 load_chunk(c + 1)
             load_old_cell(c)
-        fc3_raw = const.tile([P, HID], BF16)
-        nc.sync.dma_start(out=fc3_raw[:], in_=fc3_w)
-        fc3_bias = const.tile([P, ACTIONS], BF16)
-        nc.sync.dma_start(out=fc3_bias[:], in_=fc3_b.partition_broadcast(P))
 
         ident_f32 = const.tile([P, P], F32)
         make_identity(nc, ident_f32[:])
@@ -182,12 +185,11 @@ def tile_actor_pa_kernel(
                         start=(n == 0),
                         stop=(n == 1),
                     )
-                k = gate * TILES + ht
                 nc.scalar.activation(
                     out=gate_t[gate][:, ht, :],
                     in_=bank[:],
                     func=GATE_FUNC[gate],
-                    bias=gate_bias[:, k : k + 1],
+                    bias=gate_bias[:, ht, gate : gate + 1],
                 )
 
         def turn_back(source_t, t):
@@ -196,7 +198,10 @@ def tile_actor_pa_kernel(
                 nc.tensor.transpose(
                     bank[:, ht * P : (ht + 1) * P], source_t[:, ht, t * P : (t + 1) * P], ident_f32[:]
                 )
-            return bank
+            return bank[:].rearrange("b (j p) -> b p j", j=TILES)
+
+        def by_column(rows):
+            return rows.rearrange("b (p j) -> b p j", j=TILES)
 
         def store_half(out, c, half, tile):
             view = out[chunk_rows(c), :].rearrange("(p t) h -> p t h", t=TILES)
@@ -209,7 +214,10 @@ def tile_actor_pa_kernel(
             for t in tiles_of(half):
                 bank = turn_back(gate_t[GATE_F], t)
                 nc.vector.tensor_tensor(
-                    out=cell[c][:, t, :], in0=bank[:], in1=raw_cx[c][:, t, :], op=ALU.mult
+                    out=by_column(cell[c][:, t, :]),
+                    in0=bank,
+                    in1=by_column(raw_cx[c][:, t, :]),
+                    op=ALU.mult,
                 )
 
         def input_times_candidate(half):
@@ -225,7 +233,10 @@ def tile_actor_pa_kernel(
             for t in tiles_of(half):
                 bank = turn_back(gate_t[GATE_I], t)
                 nc.vector.tensor_tensor(
-                    out=cell[c][:, t, :], in0=bank[:], in1=cell[c][:, t, :], op=ALU.add
+                    out=by_column(cell[c][:, t, :]),
+                    in0=bank,
+                    in1=by_column(cell[c][:, t, :]),
+                    op=ALU.add,
                 )
             store_half(out_2, c, half, cell[c])
 
@@ -241,7 +252,10 @@ def tile_actor_pa_kernel(
             for t in tiles_of(half):
                 bank = turn_back(gate_t[GATE_O], t)
                 nc.vector.tensor_tensor(
-                    out=hidden[c][:, t, :], in0=bank[:], in1=hidden[c][:, t, :], op=ALU.mult
+                    out=by_column(hidden[c][:, t, :]),
+                    in0=bank,
+                    in1=by_column(hidden[c][:, t, :]),
+                    op=ALU.mult,
                 )
             store_half(out_1, c, half, hidden[c])
             for t in tiles_of(half):
@@ -282,18 +296,20 @@ def tile_actor_pa_kernel(
             for n in range(2):
                 quantise(first_x[n], x_mx[0][n], half)
 
-        bias_bank = psum_tr.tile([P, P], BF16, tag="tr", name="bias_bank")
-        nc.tensor.transpose(bias_bank[:], bias_rows[:], ident_bf16[:])
-        bias_cols = const.tile([P, 32], F32)
-        nc.vector.tensor_copy(out=bias_cols[:], in_=bias_bank[:, 0:32])
-        gate_bias = const.tile([P, 16], F32)
-        nc.vector.tensor_tensor(
-            out=gate_bias[:], in0=bias_cols[:, 0:16], in1=bias_cols[:, 16:32], op=ALU.add
-        )
-
         for half in range(2):
             quantise_weights(regroup_weights(GATE_F, half), GATE_F, half)
 
+        bias_bank = psum_tr.tile([P, TILES, P], BF16, tag="tr", name="bias_bank")
+        for j in range(TILES):
+            nc.tensor.transpose(bias_bank[:, j, :], bias_rows[:, j::TILES], ident_bf16[:])
+        bias_cols = const.tile([P, TILES, 8], F32)
+        nc.vector.tensor_copy(out=bias_cols[:], in_=bias_bank[:, :, 0:8])
+        gate_bias = const.tile([P, TILES, 4], F32)
+        nc.vector.tensor_tensor(
+            out=gate_bias[:], in0=bias_cols[:, :, 0:4], in1=bias_cols[:, :, 4:8], op=ALU.add
+        )
+
+        fc3_bias = const.tile([P, ACTIONS], F32)
         fc3_grouped = const.tile([P, ACTIONS * PACK], BF16, align_bytes=64)
         fc3_mx = new_operand("fc3", ACTIONS)
 
@@ -331,21 +347,6 @@ def tile_actor_pa_kernel(
                 if after:
                     quantise(grouped_x, x_mx[c + 1][0], half)
 
-            if c == 1:
-                fc3_words = fc3_raw[:].bitcast(F32)
-                fc3_bank = psum_tr.tile([P, 2, ACTIONS], F32, tag="tr", name="fc3_bank")
-                for u in range(2):
-                    nc.tensor.transpose(
-                        fc3_bank[:, u, :], fc3_words[:, u * P : (u + 1) * P], ident_f32[:]
-                    )
-                nc.vector.tensor_copy(
-                    out=fc3_grouped[:].bitcast(F32).rearrange("p (r u) -> p r u", u=2),
-                    in_=fc3_bank[:].rearrange("p u r -> p r u"),
-                )
-                nc.vector.quantize_mx(
-                    out=fc3_mx[0][:].bitcast(FP8X4), scales=fc3_mx[1][:], in_=fc3_grouped[:]
-                )
-
             for half in range(2):
                 if now:
                     gate_passes(c, GATE_G, half)
@@ -372,3 +373,27 @@ def tile_actor_pa_kernel(
                     squash_cell(c, 0)
                 if now:
                     new_cell(c, half)
+
+            if first:
+                fc3_bias_bank = psum_tr.tile([P, ACTIONS], F32, tag="tr", name="fc3_bias_bank")
+                nc.tensor.matmul(
+                    fc3_bias_bank[:],
+                    lhsT=ident_bf16[:, 8:9].to_broadcast([P, P]),
+                    rhs=bias_rows[:, 0:ACTIONS],
+                    start=True,
+                    stop=True,
+                )
+                nc.vector.tensor_copy(out=fc3_bias[:], in_=fc3_bias_bank[:])
+                fc3_words = fc3_raw[:].bitcast(F32)
+                fc3_bank = psum_tr.tile([P, 2, ACTIONS], F32, tag="tr", name="fc3_bank")
+                for u in range(2):
+                    nc.tensor.transpose(
+                        fc3_bank[:, u, :], fc3_words[:, u * P : (u + 1) * P], ident_f32[:]
+                    )
+                nc.vector.tensor_copy(
+                    out=fc3_grouped[:].bitcast(F32).rearrange("p (r u) -> p r u", u=2),
+                    in_=fc3_bank[:].rearrange("p u r -> p r u"),
+                )
+                nc.vector.quantize_mx(
+                    out=fc3_mx[0][:].bitcast(FP8X4), scales=fc3_mx[1][:], in_=fc3_grouped[:]
+                )

@@ -61,11 +61,11 @@ def tile_actor_pa_kernel(
             nc.sync.dma_start(out=raw[:], in_=rows.rearrange("(p t) k -> p t k", t=TILES))
             return raw
 
-        bias_rows = const.tile([P, HID], BF16)
+        bias_rows = const.tile([P, P], BF16)
         nc.vector.memset(bias_rows[:], 0.0)
-        nc.scalar.dma_start(out=bias_rows[0:4, :], in_=b_ih.rearrange("(g c) -> g c", c=HID))
-        nc.scalar.dma_start(out=bias_rows[4:8, :], in_=b_hh.rearrange("(g c) -> g c", c=HID))
-        nc.scalar.dma_start(out=bias_rows[8:9, 0:ACTIONS], in_=fc3_b.unsqueeze(0))
+        nc.scalar.dma_start(out=bias_rows[0:16, :], in_=b_ih.rearrange("(r c) -> r c", c=P))
+        nc.scalar.dma_start(out=bias_rows[16:32, :], in_=b_hh.rearrange("(r c) -> r c", c=P))
+        nc.scalar.dma_start(out=bias_rows[32:33, :], in_=fc3_b.unsqueeze(0))
         fc3_raw = const.tile([P, HID], BF16)
 
         raw_x = {}
@@ -81,28 +81,33 @@ def tile_actor_pa_kernel(
         def load_old_cell(c):
             raw_cx[c] = load_batch_rows("raw_cx%d" % c, cx[chunk_rows(c), :])
 
-        def load_in_halves(name, pair, rows):
-            raw = [loaded.tile([P, TILES, HID], BF16, name="%s_%d" % (name, n)) for n in range(2)]
+        def load_first_chunk():
+            raw_x[0] = [loaded.tile([P, TILES, HID], BF16, name="raw_x0_%d" % n) for n in range(2)]
             for half in range(2):
                 part = slice(half * HALF, (half + 1) * HALF)
-                for n in range(2):
-                    view = pair[n][rows, :].rearrange("(p t) k -> p t k", t=TILES)
-                    nc.sync.dma_start(out=raw[n][:, part, :], in_=view[:, part, :])
-            return raw
+                for raw, x in zip(raw_x[0], (h_fc2, hx)):
+                    view = x[chunk_rows(0), :].rearrange("(p t) k -> p t k", t=TILES)
+                    nc.sync.dma_start(out=raw[:, part, :], in_=view[:, part, :])
 
-        def load_gate(gate):
-            raw_w[gate] = (
-                load_batch_rows("raw_wih%d" % gate, w_ih[gate_rows(gate), :]),
-                load_batch_rows("raw_whh%d" % gate, w_hh[gate_rows(gate), :]),
-            )
+        def load_gate(gate, parts):
+            raw_w[gate] = [
+                loaded.tile([P, TILES, HID], BF16, name="raw_w%d_%d" % (gate, n)) for n in range(2)
+            ]
+            for part in range(parts):
+                halves = slice(part * 2 // parts, (part + 1) * 2 // parts)
+                tiles = slice(halves.start * HALF, halves.stop * HALF)
+                for raw, w in zip(raw_w[gate], (w_ih, w_hh)):
+                    view = w[gate_rows(gate), :].rearrange("(h p t) k -> p h t k", h=2, t=HALF)
+                    out = raw[:, tiles, :].rearrange("p (h t) k -> p h t k", t=HALF)
+                    nc.sync.dma_start(out=out, in_=view[:, halves, :, :])
 
-        raw_x[0] = load_in_halves("raw_x0", (h_fc2, hx), chunk_rows(0))
-        raw_w[GATE_F] = load_in_halves("raw_wf", (w_ih, w_hh), gate_rows(GATE_F))
-        load_gate(GATE_I)
-        load_gate(GATE_G)
+        load_first_chunk()
+        load_gate(GATE_F, 2)
+        load_gate(GATE_I, 1)
+        load_gate(GATE_G, 1)
         load_old_cell(0)
         load_chunk(1)
-        load_gate(GATE_O)
+        load_gate(GATE_O, 1)
         nc.sync.dma_start(out=fc3_raw[:], in_=fc3_w)
         for c in range(1, N_CHUNKS):
             if c + 1 < N_CHUNKS:
@@ -123,7 +128,7 @@ def tile_actor_pa_kernel(
             scales = operands.tile([P, columns], U8, align_bytes=64, name="scales_" + name)
             return codes, scales
 
-        def regroup(raw, half, engine):
+        def regroup(raw, half, engine, rows_in_turn=False):
             words = raw[:].rearrange("p t k -> p (t k)").bitcast(F32)
             words = words.rearrange("p (t w) -> p t w", t=TILES)
             bank = psum_tr.tile([P, 2, HALF * P], F32, tag="tr", name="word_bank")
@@ -133,11 +138,16 @@ def tile_actor_pa_kernel(
                         bank[:, u, j * P : (j + 1) * P], words[:, t, u * P : (u + 1) * P], ident_f32[:]
                     )
             grouped = stage.tile([P, HALF * P * PACK], BF16, align_bytes=64, name="grouped")
-            grouped_words = grouped[:].bitcast(F32).rearrange("p (r u) -> p r u", u=2)
-            if engine == "scalar":
-                nc.scalar.copy(out=grouped_words, in_=bank[:].rearrange("p u r -> p r u"))
+            if rows_in_turn:
+                out = grouped[:].bitcast(F32).rearrange("p (r j u) -> p r j u", j=HALF, u=2)
+                in_ = bank[:].rearrange("p u (j r) -> p r j u", j=HALF)
             else:
-                nc.vector.tensor_copy(out=grouped_words, in_=bank[:].rearrange("p u r -> p r u"))
+                out = grouped[:].bitcast(F32).rearrange("p (r u) -> p r u", u=2)
+                in_ = bank[:].rearrange("p u r -> p r u")
+            if engine == "scalar":
+                nc.scalar.copy(out=out, in_=in_)
+            else:
+                nc.vector.tensor_copy(out=out, in_=in_)
             return grouped
 
         def quantise(grouped, operand, half):
@@ -154,8 +164,8 @@ def tile_actor_pa_kernel(
             if half == 0:
                 w_mx[gate] = [new_operand("w%d_%d" % (gate, n), HID) for n in range(2)]
             return [
-                regroup(raw_w[gate][0], half, "scalar"),
-                regroup(raw_w[gate][1], half, "vector"),
+                regroup(raw_w[gate][0], half, "scalar", rows_in_turn=True),
+                regroup(raw_w[gate][1], half, "vector", rows_in_turn=True),
             ]
 
         def quantise_weights(grouped, gate, half):
@@ -185,11 +195,12 @@ def tile_actor_pa_kernel(
                         start=(n == 0),
                         stop=(n == 1),
                     )
+                k = gate * TILES + ht
                 nc.scalar.activation(
                     out=gate_t[gate][:, ht, :],
                     in_=bank[:],
                     func=GATE_FUNC[gate],
-                    bias=gate_bias[:, ht, gate : gate + 1],
+                    bias=gate_bias[:, k : k + 1],
                 )
 
         def turn_back(source_t, t):
@@ -198,10 +209,7 @@ def tile_actor_pa_kernel(
                 nc.tensor.transpose(
                     bank[:, ht * P : (ht + 1) * P], source_t[:, ht, t * P : (t + 1) * P], ident_f32[:]
                 )
-            return bank[:].rearrange("b (j p) -> b p j", j=TILES)
-
-        def by_column(rows):
-            return rows.rearrange("b (p j) -> b p j", j=TILES)
+            return bank
 
         def store_half(out, c, half, tile):
             view = out[chunk_rows(c), :].rearrange("(p t) h -> p t h", t=TILES)
@@ -214,10 +222,7 @@ def tile_actor_pa_kernel(
             for t in tiles_of(half):
                 bank = turn_back(gate_t[GATE_F], t)
                 nc.vector.tensor_tensor(
-                    out=by_column(cell[c][:, t, :]),
-                    in0=bank,
-                    in1=by_column(raw_cx[c][:, t, :]),
-                    op=ALU.mult,
+                    out=cell[c][:, t, :], in0=bank[:], in1=raw_cx[c][:, t, :], op=ALU.mult
                 )
 
         def input_times_candidate(half):
@@ -233,10 +238,7 @@ def tile_actor_pa_kernel(
             for t in tiles_of(half):
                 bank = turn_back(gate_t[GATE_I], t)
                 nc.vector.tensor_tensor(
-                    out=by_column(cell[c][:, t, :]),
-                    in0=bank,
-                    in1=by_column(cell[c][:, t, :]),
-                    op=ALU.add,
+                    out=cell[c][:, t, :], in0=bank[:], in1=cell[c][:, t, :], op=ALU.add
                 )
             store_half(out_2, c, half, cell[c])
 
@@ -252,10 +254,7 @@ def tile_actor_pa_kernel(
             for t in tiles_of(half):
                 bank = turn_back(gate_t[GATE_O], t)
                 nc.vector.tensor_tensor(
-                    out=by_column(hidden[c][:, t, :]),
-                    in0=bank,
-                    in1=by_column(hidden[c][:, t, :]),
-                    op=ALU.mult,
+                    out=hidden[c][:, t, :], in0=bank[:], in1=hidden[c][:, t, :], op=ALU.mult
                 )
             store_half(out_1, c, half, hidden[c])
             for t in tiles_of(half):
@@ -299,14 +298,13 @@ def tile_actor_pa_kernel(
         for half in range(2):
             quantise_weights(regroup_weights(GATE_F, half), GATE_F, half)
 
-        bias_bank = psum_tr.tile([P, TILES, P], BF16, tag="tr", name="bias_bank")
-        for j in range(TILES):
-            nc.tensor.transpose(bias_bank[:, j, :], bias_rows[:, j::TILES], ident_bf16[:])
-        bias_cols = const.tile([P, TILES, 8], F32)
-        nc.vector.tensor_copy(out=bias_cols[:], in_=bias_bank[:, :, 0:8])
-        gate_bias = const.tile([P, TILES, 4], F32)
+        bias_bank = psum_tr.tile([P, P], BF16, tag="tr", name="bias_bank")
+        nc.tensor.transpose(bias_bank[:], bias_rows[:], ident_bf16[:])
+        bias_cols = const.tile([P, 32], F32)
+        nc.vector.tensor_copy(out=bias_cols[:], in_=bias_bank[:, 0:32])
+        gate_bias = const.tile([P, 16], F32)
         nc.vector.tensor_tensor(
-            out=gate_bias[:], in0=bias_cols[:, :, 0:4], in1=bias_cols[:, :, 4:8], op=ALU.add
+            out=gate_bias[:], in0=bias_cols[:, 0:16], in1=bias_cols[:, 16:32], op=ALU.add
         )
 
         fc3_bias = const.tile([P, ACTIONS], F32)
@@ -378,8 +376,8 @@ def tile_actor_pa_kernel(
                 fc3_bias_bank = psum_tr.tile([P, ACTIONS], F32, tag="tr", name="fc3_bias_bank")
                 nc.tensor.matmul(
                     fc3_bias_bank[:],
-                    lhsT=ident_bf16[:, 8:9].to_broadcast([P, P]),
-                    rhs=bias_rows[:, 0:ACTIONS],
+                    lhsT=ident_bf16[:, 32:33].to_broadcast([P, P]),
+                    rhs=bias_rows[:],
                     start=True,
                     stop=True,
                 )

@@ -203,6 +203,45 @@ def tile_actor_pa_kernel(
                     bias=gate_bias[:, k : k + 1],
                 )
 
+        def gate_passes_by_rows(c, gate, part):
+            if part == 0:
+                gate_t[gate] = gates_t.tile([P, TILES, CHUNK], F32, name="gate_t%d" % gate)
+            rows = slice(part * HALF * P, (part + 1) * HALF * P)
+            for pair in range(2):
+                bank = psum_mx.tile([P, 2, HALF * P], F32, tag="mx", name="gate_bank")
+                for j in range(2):
+                    ht = 2 * pair + j
+                    cols = slice(ht * P, (ht + 1) * P)
+                    for n in range(2):
+                        nc.tensor.matmul_mx(
+                            out=bank[:, j, :],
+                            lhsT=w_mx[gate][n][0][:, cols].bitcast(FP8X4),
+                            lhsT_scale=w_mx[gate][n][1][:, cols],
+                            rhs=x_mx[c][n][0][:, rows].bitcast(FP8X4),
+                            rhs_scale=x_mx[c][n][1][:, rows],
+                            start=(n == 0),
+                            stop=(n == 1),
+                        )
+                for j in range(2):
+                    ht = 2 * pair + j
+                    nc.scalar.activation(
+                        out=gate_t[gate][:, ht, rows],
+                        in_=bank[:, j, :],
+                        func=GATE_FUNC[gate],
+                        bias=gate_bias[:, gate * TILES + ht : gate * TILES + ht + 1],
+                    )
+
+        def input_times_candidate_by_rows(part):
+            rows = slice(part * HALF * P, (part + 1) * HALF * P)
+            for half in range(2):
+                hts = slice(half * HALF, (half + 1) * HALF)
+                nc.vector.tensor_tensor(
+                    out=gate_t[GATE_I][:, hts, rows],
+                    in0=gate_t[GATE_I][:, hts, rows],
+                    in1=gate_t[GATE_G][:, hts, rows],
+                    op=ALU.mult,
+                )
+
         def turn_back(source_t, t):
             bank = psum_tr.tile([P, HID], F32, tag="tr", name="turned_bank")
             for ht in range(TILES):
@@ -258,7 +297,14 @@ def tile_actor_pa_kernel(
                 )
             store_half(out_1, c, half, hidden[c])
             for t in tiles_of(half):
-                nc.vector.tensor_copy(out=rounded[c][:, t, :], in_=hidden[c][:, t, :])
+                nc.gpsimd.tensor_scalar(
+                    out=rounded[c][:, t, :],
+                    in0=hidden[c][:, t, :],
+                    scalar1=1.0,
+                    scalar2=0.0,
+                    op0=ALU.mult,
+                    op1=ALU.add,
+                )
 
         def action_head(c, half):
             if half == 0:
@@ -311,8 +357,9 @@ def tile_actor_pa_kernel(
         fc3_grouped = const.tile([P, ACTIONS * PACK], BF16, align_bytes=64)
         fc3_mx = new_operand("fc3", ACTIONS)
 
-        for c in range(N_CHUNKS + 1):
-            now = c < N_CHUNKS
+        for c in range(N_CHUNKS):
+            now = True
+            last = c == N_CHUNKS - 1
             first = c == 0
             before = c > 0
             after = c + 1 < N_CHUNKS
@@ -346,13 +393,16 @@ def tile_actor_pa_kernel(
                     quantise(grouped_x, x_mx[c + 1][0], half)
 
             for half in range(2):
-                if now:
+                if last:
+                    gate_passes_by_rows(c, GATE_G, half)
+                    input_times_candidate_by_rows(half)
+                else:
                     gate_passes(c, GATE_G, half)
                     input_times_candidate(half)
                 if first:
                     grouped_w = regroup_weights(GATE_O, half)
                 if before:
-                    grouped_h = regroup(rounded[c - 1], half, "scalar")
+                    grouped_h = regroup(rounded[c - 1], half, ("vector", "scalar")[half])
                 if after:
                     grouped_x = regroup(raw_x[c + 1][1], half, "scalar")
                 if first:
@@ -363,6 +413,14 @@ def tile_actor_pa_kernel(
                     quantise(grouped_x, x_mx[c + 1][1], half)
 
             for half in range(2):
+                if last:
+                    gate_passes_by_rows(c, GATE_O, half)
+                    if half == 0:
+                        action_head(c - 1, 0)
+                        new_cell(c, 0)
+                        new_cell(c, 1)
+                    squash_cell(c, half)
+                    continue
                 if now:
                     gate_passes(c, GATE_O, half)
                 if before:
@@ -395,3 +453,13 @@ def tile_actor_pa_kernel(
                 nc.vector.quantize_mx(
                     out=fc3_mx[0][:].bitcast(FP8X4), scales=fc3_mx[1][:], in_=fc3_grouped[:]
                 )
+
+        last = N_CHUNKS - 1
+        hidden_mx[last] = new_operand("hidden", CHUNK)
+        new_hidden(last, 0)
+        action_head(last - 1, 1)
+        new_hidden(last, 1)
+        grouped_h = [regroup(rounded[last], half, "scalar") for half in range(2)]
+        for half in range(2):
+            quantise(grouped_h[half], hidden_mx[last], half)
+            action_head(last, half)

@@ -104,10 +104,10 @@ def tile_actor_pa_kernel(
         load_first_chunk()
         load_gate(GATE_F, 2)
         load_gate(GATE_I, 1)
-        load_gate(GATE_G, 1)
         load_old_cell(0)
-        load_chunk(1)
+        load_gate(GATE_G, 1)
         load_gate(GATE_O, 1)
+        load_chunk(1)
         nc.sync.dma_start(out=fc3_raw[:], in_=fc3_w)
         for c in range(1, N_CHUNKS):
             if c + 1 < N_CHUNKS:
@@ -124,8 +124,8 @@ def tile_actor_pa_kernel(
         nc.scalar.activation(out=warm[:], in_=warm[:], func=FUNC.Sigmoid)
 
         def new_operand(name, columns):
-            codes = operands.tile([P, columns], U32, align_bytes=64, name="codes_" + name)
-            scales = operands.tile([P, columns], U8, align_bytes=64, name="scales_" + name)
+            codes = operands.tile([P, columns], U32, align_bytes=256, name="codes_" + name)
+            scales = operands.tile([P, columns], U8, align_bytes=256, name="scales_" + name)
             return codes, scales
 
         def regroup(raw, half, engine, rows_in_turn=False):
@@ -385,11 +385,11 @@ def tile_actor_pa_kernel(
                     grouped_w = regroup_weights(GATE_G, half)
                 if now:
                     forget_old_cell(c, half)
-                if after:
+                if after and not first:
                     grouped_x = regroup(raw_x[c + 1][0], half, "scalar")
                 if first:
                     quantise_weights(grouped_w, GATE_G, half)
-                if after:
+                if after and not first:
                     quantise(grouped_x, x_mx[c + 1][0], half)
 
             for half in range(2):
@@ -404,13 +404,13 @@ def tile_actor_pa_kernel(
                 if before:
                     grouped_h = regroup(rounded[c - 1], half, ("vector", "scalar")[half])
                 if after:
-                    grouped_x = regroup(raw_x[c + 1][1], half, "scalar")
+                    grouped_x = regroup(raw_x[c + 1][0 if first else 1], half, "scalar")
                 if first:
                     quantise_weights(grouped_w, GATE_O, half)
                 if before:
                     quantise(grouped_h, hidden_mx[c - 1], half)
                 if after:
-                    quantise(grouped_x, x_mx[c + 1][1], half)
+                    quantise(grouped_x, x_mx[c + 1][0 if first else 1], half)
 
             for half in range(2):
                 if last:
@@ -427,8 +427,13 @@ def tile_actor_pa_kernel(
                     action_head(c - 1, half)
                 if now and half == 1:
                     squash_cell(c, 0)
+                if first and half == 0:
+                    grouped_x = [regroup(raw_x[1][1], part, "scalar") for part in range(2)]
                 if now:
                     new_cell(c, half)
+                if first and half == 0:
+                    for part in range(2):
+                        quantise(grouped_x[part], x_mx[1][1], part)
 
             if first:
                 fc3_bias_bank = psum_tr.tile([P, ACTIONS], F32, tag="tr", name="fc3_bias_bank")

from contextlib import ExitStack

import concourse.mybir as mybir
from concourse.masks import make_identity

F32 = mybir.dt.float32
BF16 = mybir.dt.bfloat16
U32 = mybir.dt.uint32
U8 = mybir.dt.uint8
FP8X4 = mybir.dt.float8_e4m3fn_x4
FUNC = mybir.ActivationFunctionType
ALU = mybir.AluOpType

P = 128
PACK = 4
HID = 512
BATCH = 2048
ACTIONS = 128
CHUNK = 512
N_CHUNKS = BATCH // CHUNK
TILES = CHUNK // P
HALF = TILES // 2
GATE_I, GATE_F, GATE_G, GATE_O = 0, 1, 2, 3
GATE_ORDER = (GATE_F, GATE_I, GATE_G, GATE_O)
GATE_FUNC = {
    GATE_I: FUNC.Sigmoid,
    GATE_F: FUNC.Sigmoid,
    GATE_G: FUNC.Tanh,
    GATE_O: FUNC.Sigmoid,
}

FLOPS = 2 * BATCH * (4 * HID) * HID * 2 + 2 * BATCH * ACTIONS * HID


def tile_actor_pa_kernel(
    tc, h_fc2, hx, cx, w_ih, w_hh, b_ih, b_hh, fc3_w, fc3_b, out_0, out_1, out_2
):
    nc = tc.nc
    with ExitStack() as stack:
        const = stack.enter_context(tc.tile_pool(name="const", bufs=1))
        loaded = stack.enter_context(tc.tile_pool(name="loaded", bufs=1))
        operands = stack.enter_context(tc.tile_pool(name="operands", bufs=1))
        stage = stack.enter_context(tc.tile_pool(name="stage", bufs=6))
        gates_t = stack.enter_context(tc.tile_pool(name="gates_t", bufs=1))
        results = stack.enter_context(tc.tile_pool(name="results", bufs=2))
        psum_mx = stack.enter_context(tc.psum_pool(name="psum_mx", bufs=3))
        psum_tr = stack.enter_context(tc.psum_pool(name="psum_tr", bufs=5))
        stack.enter_context(tc.manual_schedule())

        def chunk_rows(c):
            return slice(c * CHUNK, (c + 1) * CHUNK)

        def gate_rows(gate):
            return slice(gate * HID, (gate + 1) * HID)

        def tiles_of(half):
            return range(half * HALF, (half + 1) * HALF)

        def load_batch_rows(name, rows):
            raw = loaded.tile([P, TILES, HID], BF16, name=name)
            nc.sync.dma_start(out=raw[:], in_=rows.rearrange("(p t) k -> p t k", t=TILES))
            return raw

        bias_rows = const.tile([P, P], BF16)
        nc.vector.memset(bias_rows[:], 0.0)
        nc.scalar.dma_start(out=bias_rows[0:16, :], in_=b_ih.rearrange("(r c) -> r c", c=P))
        nc.scalar.dma_start(out=bias_rows[16:32, :], in_=b_hh.rearrange("(r c) -> r c", c=P))
        nc.scalar.dma_start(out=bias_rows[32:33, :], in_=fc3_b.unsqueeze(0))
        fc3_raw = const.tile([P, HID], BF16)

        raw_x = {}
        raw_w = {}
        raw_cx = {}

        def load_chunk(c):
            raw_x[c] = (
                load_batch_rows("raw_in%d" % c, h_fc2[chunk_rows(c), :]),
                load_batch_rows("raw_hx%d" % c, hx[chunk_rows(c), :]),
            )

        def load_old_cell(c):
            raw_cx[c] = load_batch_rows("raw_cx%d" % c, cx[chunk_rows(c), :])

        def load_first_chunk():
            raw_x[0] = [loaded.tile([P, TILES, HID], BF16, name="raw_x0_%d" % n) for n in range(2)]
            for half in range(2):
                part = slice(half * HALF, (half + 1) * HALF)
                for raw, x in zip(raw_x[0], (h_fc2, hx)):
                    view = x[chunk_rows(0), :].rearrange("(p t) k -> p t k", t=TILES)
                    nc.sync.dma_start(out=raw[:, part, :], in_=view[:, part, :])

        def load_gate(gate, parts):
            raw_w[gate] = [
                loaded.tile([P, TILES, HID], BF16, name="raw_w%d_%d" % (gate, n)) for n in range(2)
            ]
            for part in range(parts):
                halves = slice(part * 2 // parts, (part + 1) * 2 // parts)
                tiles = slice(halves.start * HALF, halves.stop * HALF)
                for raw, w in zip(raw_w[gate], (w_ih, w_hh)):
                    view = w[gate_rows(gate), :].rearrange("(h p t) k -> p h t k", h=2, t=HALF)
                    out = raw[:, tiles, :].rearrange("p (h t) k -> p h t k", t=HALF)
                    nc.sync.dma_start(out=out, in_=view[:, halves, :, :])

        load_first_chunk()
        load_gate(GATE_F, 2)
        load_gate(GATE_I, 1)
        load_old_cell(0)
        load_gate(GATE_G, 1)
        load_gate(GATE_O, 1)
        load_chunk(1)
        nc.sync.dma_start(out=fc3_raw[:], in_=fc3_w)
        for c in range(1, N_CHUNKS):
            if c + 1 < N_CHUNKS:
                load_chunk(c + 1)
            load_old_cell(c)

        ident_f32 = const.tile([P, P], F32)
        make_identity(nc, ident_f32[:])
        ident_bf16 = const.tile([P, P], BF16)
        make_identity(nc, ident_bf16[:])

        warm = const.tile([P, 1], F32)
        nc.vector.memset(warm[:], 0.0)
        nc.scalar.activation(out=warm[:], in_=warm[:], func=FUNC.Sigmoid)

        def new_operand(name, columns):
            codes = operands.tile([P, columns], U32, align_bytes=256, name="codes_" + name)
            scales = operands.tile([P, columns], U8, align_bytes=256, name="scales_" + name)
            return codes, scales

        def regroup(raw, half, engine, rows_in_turn=False):
            words = raw[:].rearrange("p t k -> p (t k)").bitcast(F32)
            words = words.rearrange("p (t w) -> p t w", t=TILES)
            bank = psum_tr.tile([P, 2, HALF * P], F32, tag="tr", name="word_bank")
            for u in range(2):
                for j, t in enumerate(tiles_of(half)):
                    nc.tensor.transpose(
                        bank[:, u, j * P : (j + 1) * P], words[:, t, u * P : (u + 1) * P], ident_f32[:]
                    )
            grouped = stage.tile([P, HALF * P * PACK], BF16, align_bytes=64, name="grouped")
            if rows_in_turn:
                out = grouped[:].bitcast(F32).rearrange("p (r j u) -> p r j u", j=HALF, u=2)
                in_ = bank[:].rearrange("p u (j r) -> p r j u", j=HALF)
            else:
                out = grouped[:].bitcast(F32).rearrange("p (r u) -> p r u", u=2)
                in_ = bank[:].rearrange("p u r -> p r u")
            if engine == "scalar":
                nc.scalar.copy(out=out, in_=in_)
            else:
                nc.vector.tensor_copy(out=out, in_=in_)
            return grouped

        def quantise(grouped, operand, half):
            codes, scales = operand
            columns = slice(half * HALF * P, (half + 1) * HALF * P)
            nc.vector.quantize_mx(
                out=codes[:, columns].bitcast(FP8X4), scales=scales[:, columns], in_=grouped[:]
            )

        x_mx = {}
        w_mx = {}

        def regroup_weights(gate, half):
            if half == 0:
                w_mx[gate] = [new_operand("w%d_%d" % (gate, n), HID) for n in range(2)]
            return [
                regroup(raw_w[gate][0], half, "scalar", rows_in_turn=True),
                regroup(raw_w[gate][1], half, "vector", rows_in_turn=True),
            ]

        def quantise_weights(grouped, gate, half):
            for n in range(2):
                quantise(grouped[n], w_mx[gate][n], half)

        gate_t = {}
        cell = {}
        hidden = {}
        rounded = {}
        hidden_mx = {}
        actions = {}

        def gate_passes(c, gate, half):
            if half == 0:
                gate_t[gate] = gates_t.tile([P, TILES, CHUNK], F32, name="gate_t%d" % gate)
            for ht in tiles_of(half):
                cols = slice(ht * P, (ht + 1) * P)
                bank = psum_mx.tile([P, CHUNK], F32, tag="mx", name="gate_bank")
                for n in range(2):
                    nc.tensor.matmul_mx(
                        out=bank[:],
                        lhsT=w_mx[gate][n][0][:, cols].bitcast(FP8X4),
                        lhsT_scale=w_mx[gate][n][1][:, cols],
                        rhs=x_mx[c][n][0][:].bitcast(FP8X4),
                        rhs_scale=x_mx[c][n][1][:],
                        start=(n == 0),
                        stop=(n == 1),
                    )
                k = gate * TILES + ht
                nc.scalar.activation(
                    out=gate_t[gate][:, ht, :],
                    in_=bank[:],
                    func=GATE_FUNC[gate],
                    bias=gate_bias[:, k : k + 1],
                )

        def gate_passes_by_rows(c, gate, part):
            if part == 0:
                gate_t[gate] = gates_t.tile([P, TILES, CHUNK], F32, name="gate_t%d" % gate)
            rows = slice(part * HALF * P, (part + 1) * HALF * P)
            for pair in range(2):
                bank = psum_mx.tile([P, 2, HALF * P], F32, tag="mx", name="gate_bank")
                for j in range(2):
                    ht = 2 * pair + j
                    cols = slice(ht * P, (ht + 1) * P)
                    for n in range(2):
                        nc.tensor.matmul_mx(
                            out=bank[:, j, :],
                            lhsT=w_mx[gate][n][0][:, cols].bitcast(FP8X4),
                            lhsT_scale=w_mx[gate][n][1][:, cols],
                            rhs=x_mx[c][n][0][:, rows].bitcast(FP8X4),
                            rhs_scale=x_mx[c][n][1][:, rows],
                            start=(n == 0),
                            stop=(n == 1),
                        )
                for j in range(2):
                    ht = 2 * pair + j
                    nc.scalar.activation(
                        out=gate_t[gate][:, ht, rows],
                        in_=bank[:, j, :],
                        func=GATE_FUNC[gate],
                        bias=gate_bias[:, gate * TILES + ht : gate * TILES + ht + 1],
                    )

        def input_times_candidate_by_rows(part):
            rows = slice(part * HALF * P, (part + 1) * HALF * P)
            for half in range(2):
                hts = slice(half * HALF, (half + 1) * HALF)
                nc.vector.tensor_tensor(
                    out=gate_t[GATE_I][:, hts, rows],
                    in0=gate_t[GATE_I][:, hts, rows],
                    in1=gate_t[GATE_G][:, hts, rows],
                    op=ALU.mult,
                )

        def turn_back(source_t, t):
            bank = psum_tr.tile([P, HID], F32, tag="tr", name="turned_bank")
            for ht in range(TILES):
                nc.tensor.transpose(
                    bank[:, ht * P : (ht + 1) * P], source_t[:, ht, t * P : (t + 1) * P], ident_f32[:]
                )
            return bank

        def store_half(out, c, half, tile):
            view = out[chunk_rows(c), :].rearrange("(p t) h -> p t h", t=TILES)
            part = slice(half * HALF, (half + 1) * HALF)
            nc.sync.dma_start(out=view[:, part, :], in_=tile[:, part, :])

        def forget_old_cell(c, half):
            if half == 0:
                cell[c] = results.tile([P, TILES, HID], F32, name="cell")
            for t in tiles_of(half):
                bank = turn_back(gate_t[GATE_F], t)
                nc.vector.tensor_tensor(
                    out=cell[c][:, t, :], in0=bank[:], in1=raw_cx[c][:, t, :], op=ALU.mult
                )

        def input_times_candidate(half):
            for ht in tiles_of(half):
                nc.vector.tensor_tensor(
                    out=gate_t[GATE_I][:, ht, :],
                    in0=gate_t[GATE_I][:, ht, :],
                    in1=gate_t[GATE_G][:, ht, :],
                    op=ALU.mult,
                )

        def new_cell(c, half):
            for t in tiles_of(half):
                bank = turn_back(gate_t[GATE_I], t)
                nc.vector.tensor_tensor(
                    out=cell[c][:, t, :], in0=bank[:], in1=cell[c][:, t, :], op=ALU.add
                )
            store_half(out_2, c, half, cell[c])

        def squash_cell(c, half):
            if half == 0:
                hidden[c] = results.tile([P, TILES, HID], F32, name="hidden")
            for t in tiles_of(half):
                nc.scalar.activation(out=hidden[c][:, t, :], in_=cell[c][:, t, :], func=FUNC.Tanh)

        def new_hidden(c, half):
            if half == 0:
                rounded[c] = results.tile([P, TILES, HID], BF16, name="rounded")
            for t in tiles_of(half):
                bank = turn_back(gate_t[GATE_O], t)
                nc.vector.tensor_tensor(
                    out=hidden[c][:, t, :], in0=bank[:], in1=hidden[c][:, t, :], op=ALU.mult
                )
            store_half(out_1, c, half, hidden[c])
            for t in tiles_of(half):
                nc.gpsimd.tensor_scalar(
                    out=rounded[c][:, t, :],
                    in0=hidden[c][:, t, :],
                    scalar1=1.0,
                    scalar2=0.0,
                    op0=ALU.mult,
                    op1=ALU.add,
                )

        def action_head(c, half):
            if half == 0:
                actions[c] = results.tile([P, TILES, ACTIONS], F32, name="actions")
            codes, scales = hidden_mx[c]
            bank = psum_mx.tile([P, HALF, ACTIONS], F32, tag="mx", name="act_bank")
            for j, t in enumerate(tiles_of(half)):
                rows = slice(t * P, (t + 1) * P)
                nc.tensor.matmul_mx(
                    out=bank[:, j, :],
                    lhsT=codes[:, rows].bitcast(FP8X4),
                    lhsT_scale=scales[:, rows],
                    rhs=fc3_mx[0][:].bitcast(FP8X4),
                    rhs_scale=fc3_mx[1][:],
                    start=True,
                    stop=True,
                )
            part = actions[c][:, half * HALF : (half + 1) * HALF, :]
            nc.vector.tensor_tensor(
                out=part,
                in0=bank[:],
                in1=fc3_bias[:].unsqueeze(1).to_broadcast([P, HALF, ACTIONS]),
                op=ALU.add,
            )
            nc.scalar.activation(out=part, in_=part, func=FUNC.Tanh)
            store_half(out_0, c, half, actions[c])

        x_mx[0] = [new_operand("x0_%d" % n, CHUNK) for n in range(2)]
        for half in range(2):
            first_x = [
                regroup(raw_x[0][0], half, "scalar"),
                regroup(raw_x[0][1], half, "vector"),
            ]
            for n in range(2):
                quantise(first_x[n], x_mx[0][n], half)

        for half in range(2):
            quantise_weights(regroup_weights(GATE_F, half), GATE_F, half)

        bias_bank = psum_tr.tile([P, P], BF16, tag="tr", name="bias_bank")
        nc.tensor.transpose(bias_bank[:], bias_rows[:], ident_bf16[:])
        bias_cols = const.tile([P, 32], F32)
        nc.vector.tensor_copy(out=bias_cols[:], in_=bias_bank[:, 0:32])
        gate_bias = const.tile([P, 16], F32)
        nc.vector.tensor_tensor(
            out=gate_bias[:], in0=bias_cols[:, 0:16], in1=bias_cols[:, 16:32], op=ALU.add
        )

        fc3_bias = const.tile([P, ACTIONS], F32)
        fc3_grouped = const.tile([P, ACTIONS * PACK], BF16, align_bytes=64)
        fc3_mx = new_operand("fc3", ACTIONS)

        for c in range(N_CHUNKS):
            now = True
            last = c == N_CHUNKS - 1
            first = c == 0
            before = c > 0
            after = c + 1 < N_CHUNKS
            if after:
                x_mx[c + 1] = [new_operand("x%d_%d" % (c + 1, n), CHUNK) for n in range(2)]
            if before:
                hidden_mx[c - 1] = new_operand("hidden", CHUNK)

            for half in range(2):
                if now:
                    gate_passes(c, GATE_F, half)
                if first:
                    quantise_weights(regroup_weights(GATE_I, half), GATE_I, half)
                if before and half == 0:
                    squash_cell(c - 1, 1)
                if before:
                    new_hidden(c - 1, half)

            for half in range(2):
                if now:
                    gate_passes(c, GATE_I, half)
                if first:
                    grouped_w = regroup_weights(GATE_G, half)
                if now:
                    forget_old_cell(c, half)
                if after and not first:
                    grouped_x = regroup(raw_x[c + 1][0], half, "scalar")
                if first:
                    quantise_weights(grouped_w, GATE_G, half)
                if after and not first:
                    quantise(grouped_x, x_mx[c + 1][0], half)

            for half in range(2):
                if last:
                    gate_passes_by_rows(c, GATE_G, half)
                    input_times_candidate_by_rows(half)
                else:
                    gate_passes(c, GATE_G, half)
                    input_times_candidate(half)
                if first:
                    grouped_w = regroup_weights(GATE_O, half)
                if before:
                    grouped_h = regroup(rounded[c - 1], half, ("vector", "scalar")[half])
                if after:
                    grouped_x = regroup(raw_x[c + 1][0 if first else 1], half, "scalar")
                if first:
                    quantise_weights(grouped_w, GATE_O, half)
                if before:
                    quantise(grouped_h, hidden_mx[c - 1], half)
                if after:
                    quantise(grouped_x, x_mx[c + 1][0 if first else 1], half)

            for half in range(2):
                if last:
                    gate_passes_by_rows(c, GATE_O, half)
                    if half == 0:
                        action_head(c - 1, 0)
                        new_cell(c, 0)
                        new_cell(c, 1)
                    squash_cell(c, half)
                    continue
                if now:
                    gate_passes(c, GATE_O, half)
                if before:
                    action_head(c - 1, half)
                if now and half == 1:
                    squash_cell(c, 0)
                if first and half == 0:
                    grouped_x = [regroup(raw_x[1][1], part, "scalar") for part in range(2)]
                if now:
                    new_cell(c, half)
                if first and half == 0:
                    for part in range(2):
                        quantise(grouped_x[part], x_mx[1][1], part)

            if first:
                fc3_bias_bank = psum_tr.tile([P, ACTIONS], F32, tag="tr", name="fc3_bias_bank")
                nc.tensor.matmul(
                    fc3_bias_bank[:],
                    lhsT=ident_bf16[:, 32:33].to_broadcast([P, P]),
                    rhs=bias_rows[:],
                    start=True,
                    stop=True,
                )
                nc.vector.tensor_copy(out=fc3_bias[:], in_=fc3_bias_bank[:])
                fc3_words = fc3_raw[:].bitcast(F32)
                fc3_bank = psum_tr.tile([P, 2, ACTIONS], F32, tag="tr", name="fc3_bank")
                for u in range(2):
                    nc.tensor.transpose(
                        fc3_bank[:, u, :], fc3_words[:, u * P : (u + 1) * P], ident_f32[:]
                    )
                nc.vector.tensor_copy(
                    out=fc3_grouped[:].bitcast(F32).rearrange("p (r u) -> p r u", u=2),
                    in_=fc3_bank[:].rearrange("p u r -> p r u"),
                )
                nc.vector.quantize_mx(
                    out=fc3_mx[0][:].bitcast(FP8X4), scales=fc3_mx[1][:], in_=fc3_grouped[:]
                )

        last = N_CHUNKS - 1
        hidden_mx[last] = new_operand("hidden", CHUNK)
        new_hidden(last, 0)
        action_head(last - 1, 1)
        new_hidden(last, 1)
        grouped_h = [regroup(rounded[last], half, "scalar") for half in range(2)]
        for half in range(2):
            quantise(grouped_h[half], hidden_mx[last], half)
            action_head(last, half)
